import numpy as np
import ml_dtypes


def mxq(x, axis, fmt="e4m3"):
    dtype, down = {"e4m3": (ml_dtypes.float8_e4m3fn, 7), "e5m2": (ml_dtypes.float8_e5m2, 14)}[fmt]
    v = np.moveaxis(np.asarray(x, np.float32).astype(ml_dtypes.bfloat16).astype(np.float64), axis, -1)
    blocks = v.reshape(v.shape[:-1] + (-1, 32))
    amax = np.abs(blocks).max(-1, keepdims=True)
    byte = np.maximum(np.where(amax > 0, np.frexp(amax)[1] - 1 + 127, 0) - down, 1)
    scale = np.exp2(byte - 127.0)
    codes = (blocks / scale).astype(np.float32).astype(dtype).astype(np.float64)
    return np.moveaxis((codes * scale).reshape(v.shape), -1, axis)


WIDE = False


def mx_kscale(k):
    if not WIDE:
        return np.ones(k)
    levels = np.array([10, -10, 5, -5, 0])
    if k % 512:
        return np.exp2(np.random.permutation(np.resize(levels, k // 32))).repeat(32)
    a = np.empty((k // 512, 16))
    for p in range(k // 512):
        a[p, :8] = np.random.permutation(np.resize(levels, 8))
        for g in range(8):
            far = levels[np.abs(levels - a[p, g]) >= 10]
            a[p, g + 8] = far[np.random.randint(len(far))]
    return np.exp2(a.ravel()).repeat(32)


BF16 = ml_dtypes.bfloat16


def bf(x):
    return np.asarray(x, np.float32).astype(BF16)


def f64(x):
    return np.asarray(x).astype(np.float64)


B, T, D, E, F, H = 2, 128, 1024, 8, 512, 256
N = B * T
EF = E * F


def silu(v):
    return v / (1.0 + np.exp(-v))


def setup_inputs():
    s = mx_kscale(D)
    t = mx_kscale(EF).reshape(E, F)
    er = np.exp(np.random.standard_normal((N, E)))
    return {"x": bf(np.random.standard_normal((B, T, D)) * s),
            "r": bf(er / er.sum(-1, keepdims=True)),
            "Wg": bf(np.random.standard_normal((E, D, F)) / np.sqrt(D) / s[None, :, None]),
            "Wu": bf(np.random.standard_normal((E, D, F)) / np.sqrt(D) / s[None, :, None] * t[:, None, :]),
            "Wd": bf(np.random.standard_normal((E, F, D)) * 1.5 / np.sqrt(F) / t[:, :, None])}


def reference(x, r, Wg, Wu, Wd):
    xq = mxq(f64(x).reshape(N, D), 1, "e4m3")
    g = silu(xq @ mxq(f64(Wg), 1, "e4m3"))
    u = xq @ mxq(f64(Wu), 1, "e4m3")
    w = f64(r).T[:, :, None] * (g * u)
    w = np.swapaxes(w, 0, 1).reshape(N, EF)
    y = mxq(w, 1, "e4m3") @ mxq(f64(Wd).reshape(EF, D), 0, "e4m3")
    return y.reshape(B, T, D)

@@ -1,0 +1,303 @@
+from contextlib import ExitStack
+
+import concourse.mybir as mybir
+from concourse.masks import make_identity
+
+F32 = mybir.dt.float32
+BF16 = mybir.dt.bfloat16
+U32 = mybir.dt.uint32
+U8 = mybir.dt.uint8
+FP8X4 = mybir.dt.float8_e4m3fn_x4
+SILU = mybir.ActivationFunctionType.Silu
+MULT = mybir.AluOpType.mult
+
+P = 128
+E = 8
+D = 1024
+F = 512
+NTOK = 256
+FLOPS = 2 * NTOK * D * F * E * 2 + 2 * NTOK * E * F * D
+
+N1 = 32
+BLOCKS = ((0, 512), (512, 256), (768, 256))
+NU = N1 + E * len(BLOCKS)
+RAW_BUFS = 16
+CV1 = 248
+CV2 = {512: 264, 256: 136}
+CV2_PE = 216
+N_PE = 38
+PE_COLS = 128
+MANUAL = True
+
+
+def tile_moelayer_pa_kernel(tc, x, r, Wg, Wu, Wd, out):
+    nc = tc.nc
+    with ExitStack() as ctx:
+        const = ctx.enter_context(tc.tile_pool(name="const", bufs=1))
+        rawa = ctx.enter_context(tc.tile_pool(name="rawa", bufs=RAW_BUFS))
+        rawd = ctx.enter_context(tc.tile_pool(name="rawd", bufs=E))
+        grp = ctx.enter_context(tc.tile_pool(name="grp", bufs=6))
+        cod = ctx.enter_context(tc.tile_pool(name="cod", bufs=8))
+        act = ctx.enter_context(tc.tile_pool(name="act", bufs=3))
+        yst = ctx.enter_context(tc.tile_pool(name="yst", bufs=6))
+        psg = ctx.enter_context(tc.psum_pool(name="psg", bufs=2))
+        psu = ctx.enter_context(tc.psum_pool(name="psu", bufs=2))
+        pst = ctx.enter_context(tc.psum_pool(name="pst", bufs=2))
+        psc = ctx.enter_context(tc.psum_pool(name="psc", bufs=2))
+        if MANUAL:
+            ctx.enter_context(tc.manual_schedule())
+
+        raw_tiles = {}
+        grp_tiles = {}
+        code_tiles = {}
+        acc = {}
+        sg_tiles = {}
+        w_tiles = {}
+        wt_tiles = {}
+        wg_tiles = {}
+        ck_tiles = {}
+
+        def load(n):
+            if n < N1:
+                e, i = divmod(n, 4)
+                src = (Wg if i < 2 else Wu)[e]
+                c = i % 2
+                t = rawa.tile([P, 4, F], BF16, name="rawa", tag="rawa")
+                nc.sync.dma_start(
+                    out=t[:], in_=src[512 * c : 512 * c + 512, :].rearrange("(p j) f -> p j f", j=4)
+                )
+                raw_tiles[n] = t
+            else:
+                e = n - N1
+                t = rawd.tile([P, 4, D], BF16, name="rawd", tag="rawd")
+                nc.sync.dma_start(out=t[:], in_=Wd[e].rearrange("(p t) d -> p t d", t=4))
+                raw_tiles[n] = t
+
+        def width(n):
+            return F if n < N1 else BLOCKS[(n - N1) // E][1]
+
+        def source(n):
+            if n < N1:
+                return raw_tiles[n][:]
+            b, e = divmod(n - N1, E)
+            return raw_tiles[N1 + e][:, :, BLOCKS[b][0] : BLOCKS[b][0] + BLOCKS[b][1]]
+
+        def split(n):
+            return CV1 if n < N1 else (CV2_PE if n < N_PE else CV2[width(n)])
+
+        def pe_regroup(n):
+            cv = split(n)
+            ck = psc.tile([P, PE_COLS, 4], BF16, name="ck", tag="ck")
+            nc.tensor.matmul(
+                out=ck[:].rearrange("p w t -> p t w"),
+                lhsT=ident_b[:],
+                rhs=source(n)[:, :, cv : cv + PE_COLS],
+                start=True,
+                stop=True,
+            )
+            ck_tiles[n] = ck
+
+        def regroup(n):
+            w = width(n)
+            g = grp.tile([P, w, 4], BF16, name="grp", tag="grp", align_bytes=64)
+            grp_tiles[n] = g
+            src = source(n)
+            cv = split(n)
+            cs = cv + PE_COLS if n < N_PE else cv
+            nc.scalar.copy(
+                out=g[:, cs:w, :].rearrange("p (c i) t -> p c t i", i=4),
+                in_=src[:, :, cs:w].rearrange("p t (c i) -> p c t i", i=4),
+            )
+            if n < N_PE:
+                nc.scalar.copy(out=g[:, cv:cs, :], in_=ck_tiles[n][:])
+            nc.vector.tensor_copy(
+                out=g[:, 0:cv, :].rearrange("p (c i) t -> p c t i", i=4),
+                in_=src[:, :, 0:cv].rearrange("p t (c i) -> p c t i", i=4),
+            )
+            nxt = n + RAW_BUFS
+            if nxt < N1:
+                load(nxt)
+            elif nxt == N1:
+                for e in range(E):
+                    load(N1 + e)
+
+        def quantise(n):
+            codes = cod.tile([P, width(n)], U32, name="codes", tag="codes", align_bytes=64)
+            plane = cod.tile([P, width(n)], U8, name="plane", tag="plane", align_bytes=64)
+            nc.vector.quantize_mx(
+                out=codes[:].bitcast(FP8X4),
+                scales=plane[:],
+                in_=grp_tiles[n][:].rearrange("p w t -> p (w t)"),
+            )
+            code_tiles[n] = (codes, plane)
+
+        ident_f = const.tile([P, P], F32, name="ident_f")
+        make_identity(nc, ident_f[:])
+        ident_b = const.tile([P, P], BF16, name="ident_b")
+        make_identity(nc, ident_b[:])
+        r_sb = const.tile([P, 2, E], BF16, name="r_sb")
+        nc.scalar.dma_start(out=r_sb[:], in_=r.rearrange("(a p) e -> p a e", a=2))
+        warm = const.tile([P, 1], F32, name="warm")
+        nc.vector.memset(warm[:], 0.0)
+        nc.scalar.activation(out=warm[:], in_=warm[:], func=SILU)
+        x_sb = const.tile([P, 2, D], BF16, name="x_sb")
+        load(0)
+        nc.sync.dma_start(out=x_sb[:], in_=x.rearrange("b t d -> t b d"))
+        for n in range(1, RAW_BUFS):
+            load(n)
+
+        r32 = const.tile([P, 2, E], F32, name="r32")
+        nc.vector.tensor_copy(out=r32[:], in_=r_sb[:])
+
+        xg = const.tile([P, 2, NTOK, 4], BF16, name="xg", align_bytes=64)
+        xc = const.tile([P, 2 * NTOK], U32, name="xc", align_bytes=64)
+        xs = const.tile([P, 2 * NTOK], U8, name="xs", align_bytes=64)
+        wc = const.tile([P, E, NTOK], U32, name="wc", align_bytes=64)
+        ws = const.tile([P, E, NTOK], U8, name="ws", align_bytes=64)
+
+        def x_transposes(c):
+            xw = x_sb[:].bitcast(F32).rearrange("p a (c q u) -> p a c u q", c=2, u=2)
+            xg32 = xg[:].bitcast(F32)
+            xt = pst.tile([P, 2, 2, P], F32, name="xt", tag="tp")
+            for a in range(2):
+                for u in range(2):
+                    nc.tensor.transpose(out=xt[:, a, u, :], in_=xw[:, a, c, u, :], identity=ident_f[:])
+            nc.scalar.copy(
+                out=xg32[:, c].rearrange("p (a q) u -> p a q u", a=2),
+                in_=xt[:].rearrange("p a u q -> p a q u"),
+            )
+
+        def x_quantise():
+            nc.vector.quantize_mx(
+                out=xc[:].bitcast(FP8X4),
+                scales=xs[:],
+                in_=xg[:].rearrange("p c n t -> p (c n t)"),
+            )
+
+        def matmuls(n):
+            codes, plane = code_tiles[n]
+            if n < N1:
+                e, i = divmod(n, 4)
+                c = i % 2
+                for a in range(2):
+                    if c == 0:
+                        pool = psg if i < 2 else psu
+                        acc[(i // 2, e, a)] = pool.tile([P, F], F32, name="acc", tag="acc")
+                    cols = slice(NTOK * c + P * a, NTOK * c + P * a + P)
+                    nc.tensor.matmul_mx(
+                        out=acc[(i // 2, e, a)][:],
+                        lhsT=xc[:, cols].bitcast(FP8X4),
+                        lhsT_scale=xs[:, cols],
+                        rhs=codes[:].bitcast(FP8X4),
+                        rhs_scale=plane[:],
+                        start=(c == 0),
+                        stop=(c == 1),
+                    )
+            else:
+                b, e = divmod(n - N1, E)
+                for a in range(2):
+                    if e == 0:
+                        pool = (psg, psu, psg)[b]
+                        acc[(2 + b, 0, a)] = pool.tile([P, BLOCKS[b][1]], F32, name="acc", tag="acc")
+                    cols = slice(P * a, P * a + P)
+                    nc.tensor.matmul_mx(
+                        out=acc[(2 + b, 0, a)][:],
+                        lhsT=wc[:, e, cols].bitcast(FP8X4),
+                        lhsT_scale=ws[:, e, cols],
+                        rhs=codes[:].bitcast(FP8X4),
+                        rhs_scale=plane[:],
+                        start=(e == 0),
+                        stop=(e == E - 1),
+                    )
+
+        def silu(e, a):
+            sg = act.tile([P, 4, P], F32, name="sg", tag="sg")
+            nc.scalar.activation(
+                out=sg[:], in_=acc[(0, e, a)][:].rearrange("p (q t) -> p t q", t=4), func=SILU
+            )
+            sg_tiles[(e, a)] = sg
+
+        def combine(e, a):
+            w = act.tile([P, 4, P], BF16, name="w", tag="w")
+            nc.vector.scalar_tensor_tensor(
+                out=w[:],
+                in0=sg_tiles[(e, a)][:],
+                scalar=r32[:, a, e : e + 1],
+                in1=acc[(1, e, a)][:].rearrange("p (q t) -> p t q", t=4),
+                op0=MULT,
+                op1=MULT,
+            )
+            w_tiles[(e, a)] = w
+
+        def w_transposes(e):
+            wt = pst.tile([P, 2, 4, P], BF16, name="wt", tag="tp")
+            for a in range(2):
+                for t in range(4):
+                    nc.tensor.transpose(
+                        out=wt[:, a, t, :], in_=w_tiles[(e, a)][:, t, :], identity=ident_b[:]
+                    )
+            wt_tiles[e] = wt
+
+        def w_copy(e, a):
+            if a == 0:
+                wg_tiles[e] = act.tile([P, NTOK, 4], BF16, name="wg", tag="wg", align_bytes=64)
+            nc.scalar.copy(
+                out=wg_tiles[e][:, P * a : P * a + P, :],
+                in_=wt_tiles[e][:, a].rearrange("p t q -> p q t"),
+            )
+
+        def w_quantise(e):
+            nc.vector.quantize_mx(
+                out=wc[:, e, :].bitcast(FP8X4),
+                scales=ws[:, e, :],
+                in_=wg_tiles[e][:].rearrange("p n t -> p (n t)"),
+            )
+
+        def y_out(b, a, copy, queue):
+            y = yst.tile([P, BLOCKS[b][1]], F32, name="y", tag="y")
+            copy(out=y[:], in_=acc[(2 + b, 0, a)][:])
+            queue.dma_start(out=out[a][:, BLOCKS[b][0] : BLOCKS[b][0] + BLOCKS[b][1]], in_=y[:])
+
+        regrouped = 0
+        pe_regroup(0)
+        pe_done = 1
+        for n in range(-1, NU):
+            ahead = 1 if n < 0 else min(n, 2)
+            while regrouped <= min(n + ahead, NU - 1):
+                regroup(regrouped)
+                if regrouped < 2:
+                    x_transposes(regrouped)
+                while pe_done <= min(regrouped + 1, N_PE - 1):
+                    pe_regroup(pe_done)
+                    pe_done += 1
+                regrouped += 1
+            if n < 0:
+                continue
+            quantise(n)
+            if n == 1:
+                x_quantise()
+                matmuls(0)
+            if n % 4 == 3 and 11 <= n <= 39:
+                w_quantise((n - 11) // 4)
+            if n >= 1:
+                matmuls(n)
+            if n < N1 and n % 4 == 2:
+                silu(n // 4, 0)
+            if n < N1 and n % 4 == 3:
+                silu(n // 4, 1)
+            if n % 4 == 0 and 8 <= n <= 36:
+                w_copy((n - 8) // 4, 0)
+            if n % 4 == 1 and 9 <= n <= 37:
+                w_copy((n - 9) // 4, 1)
+            for b in range(len(BLOCKS) - 1):
+                if n == N1 + E * b + E + 1:
+                    y_out(b, 0, nc.scalar.copy, nc.sync)
+                if n == N1 + E * b + E + 2:
+                    y_out(b, 1, nc.scalar.copy, nc.sync)
+            if n % 4 == 0 and 4 <= n <= 32:
+                combine((n - 4) // 4, 0)
+            if n % 4 == 1 and 5 <= n <= 33:
+                combine((n - 5) // 4, 1)
+                w_transposes((n - 5) // 4)
+        y_out(len(BLOCKS) - 1, 0, nc.vector.tensor_copy, nc.sync)
+        y_out(len(BLOCKS) - 1, 1, nc.scalar.copy, nc.scalar)

@@ -211,39 +211,36 @@ def tile_moelayer_pa_kernel(tc, x, r, Wg, Wu, Wd, out):
                     )
 
         def silu(e, a):
-            sg = act.tile([P, 4, P], F32, name="sg", tag="sg")
-            nc.scalar.activation(
-                out=sg[:], in_=acc[(0, e, a)][:].rearrange("p (q t) -> p t q", t=4), func=SILU
-            )
+            sg = act.tile([P, F], F32, name="sg", tag="sg")
+            nc.scalar.activation(out=sg[:], in_=acc[(0, e, a)][:], func=SILU)
             sg_tiles[(e, a)] = sg
 
         def combine(e, a):
-            w = act.tile([P, 4, P], BF16, name="w", tag="w")
+            w = act.tile([P, F], BF16, name="w", tag="w")
             nc.vector.scalar_tensor_tensor(
                 out=w[:],
                 in0=sg_tiles[(e, a)][:],
                 scalar=r32[:, a, e : e + 1],
-                in1=acc[(1, e, a)][:].rearrange("p (q t) -> p t q", t=4),
+                in1=acc[(1, e, a)][:],
                 op0=MULT,
                 op1=MULT,
             )
             w_tiles[(e, a)] = w
 
         def w_transposes(e):
-            wt = pst.tile([P, 2, 4, P], BF16, name="wt", tag="tp")
+            wt = pst.tile([P, 2, 2, P], F32, name="wt", tag="tp")
             for a in range(2):
-                for t in range(4):
-                    nc.tensor.transpose(
-                        out=wt[:, a, t, :], in_=w_tiles[(e, a)][:, t, :], identity=ident_b[:]
-                    )
+                words = w_tiles[(e, a)][:].bitcast(F32).rearrange("p (q u) -> p u q", u=2)
+                for u in range(2):
+                    nc.tensor.transpose(out=wt[:, a, u, :], in_=words[:, u, :], identity=ident_f[:])
             wt_tiles[e] = wt
 
         def w_copy(e, a):
             if a == 0:
                 wg_tiles[e] = act.tile([P, NTOK, 4], BF16, name="wg", tag="wg", align_bytes=64)
             nc.scalar.copy(
-                out=wg_tiles[e][:, P * a : P * a + P, :],
-                in_=wt_tiles[e][:, a].rearrange("p t q -> p q t"),
+                out=wg_tiles[e][:].bitcast(F32)[:, P * a : P * a + P, :],
+                in_=wt_tiles[e][:, a].rearrange("p u q -> p q u"),
             )
 
         def w_quantise(e):

@@ -22,9 +22,9 @@ N1 = 32
 BLOCKS = ((0, 512), (512, 256), (768, 256))
 NU = N1 + E * len(BLOCKS)
 RAW_BUFS = 16
-CV1 = 248
-CV2 = {512: 264, 256: 136}
-CV2_PE = 216
+CV1 = 224
+CV2 = {512: 248, 256: 128}
+CV2_PE = 200
 N_PE = 38
 PE_COLS = 128
 MANUAL = True

@@ -270,6 +270,11 @@ def tile_moelayer_pa_kernel(tc, x, r, Wg, Wu, Wd, out):
                 regrouped += 1
             if n < 0:
                 continue
+            if n % 4 == 1 and 5 <= n <= 33:
+                combine((n - 5) // 4, 0)
+            if n % 4 == 2 and 6 <= n <= 34:
+                combine((n - 6) // 4, 1)
+                w_transposes((n - 6) // 4)
             quantise(n)
             if n == 1:
                 x_quantise()
@@ -291,10 +296,5 @@ def tile_moelayer_pa_kernel(tc, x, r, Wg, Wu, Wd, out):
                     y_out(b, 0, nc.scalar.copy, nc.sync)
                 if n == N1 + E * b + E + 2:
                     y_out(b, 1, nc.scalar.copy, nc.sync)
-            if n % 4 == 0 and 4 <= n <= 32:
-                combine((n - 4) // 4, 0)
-            if n % 4 == 1 and 5 <= n <= 33:
-                combine((n - 5) // 4, 1)
-                w_transposes((n - 5) // 4)
         y_out(len(BLOCKS) - 1, 0, nc.vector.tensor_copy, nc.sync)
         y_out(len(BLOCKS) - 1, 1, nc.scalar.copy, nc.scalar)

@@ -89,9 +89,9 @@ def tile_moelayer_pa_kernel(tc, x, r, Wg, Wu, Wd, out):
             cv = split(n)
             ck = psc.tile([P, PE_COLS, 4], BF16, name="ck", tag="ck")
             nc.tensor.matmul(
-                out=ck[:].rearrange("p w t -> p t w"),
+                out=ck[:].rearrange("p w (u v) -> p u w v", u=2),
                 lhsT=ident_b[:],
-                rhs=source(n)[:, :, cv : cv + PE_COLS],
+                rhs=source(n)[:, :, cv : cv + PE_COLS].rearrange("p (u v) w -> p u w v", u=2),
                 start=True,
                 stop=True,
             )

@@ -22,9 +22,9 @@ N1 = 32
 BLOCKS = ((0, 512), (512, 256), (768, 256))
 NU = N1 + E * len(BLOCKS)
 RAW_BUFS = 16
-CV1 = 224
-CV2 = {512: 248, 256: 128}
-CV2_PE = 200
+CV1 = 216
+CV2 = {512: 264, 256: 136}
+CV2_PE = 216
 N_PE = 38
 PE_COLS = 128
 MANUAL = True

@@ -20,12 +20,16 @@ FLOPS = 2 * NTOK * D * F * E * 2 + 2 * NTOK * E * F * D
 
 N1 = 32
 BLOCKS = ((0, 512), (512, 256), (768, 256))
-NU = N1 + E * len(BLOCKS)
+EARLY = 3
+ORDER0 = [(0, e) for e in range(E)]
+ORDER1 = [(1, e) for e in range(E)]
+UNITS2 = ORDER0[: E - EARLY] + ORDER1[:EARLY] + ORDER0[E - EARLY :] + ORDER1[EARLY:] + [(2, e) for e in range(E)]
+NU = N1 + len(UNITS2)
 RAW_BUFS = 16
 CV1 = 216
 CV2 = {512: 264, 256: 136}
-CV2_PE = 216
-N_PE = 38
+CV2_PE = 208
+E_PE = 6
 PE_COLS = 128
 MANUAL = True
 
@@ -74,16 +78,21 @@ def tile_moelayer_pa_kernel(tc, x, r, Wg, Wu, Wd, out):
                 raw_tiles[n] = t
 
         def width(n):
-            return F if n < N1 else BLOCKS[(n - N1) // E][1]
+            return F if n < N1 else BLOCKS[UNITS2[n - N1][0]][1]
 
         def source(n):
             if n < N1:
                 return raw_tiles[n][:]
-            b, e = divmod(n - N1, E)
+            b, e = UNITS2[n - N1]
             return raw_tiles[N1 + e][:, :, BLOCKS[b][0] : BLOCKS[b][0] + BLOCKS[b][1]]
 
         def split(n):
-            return CV1 if n < N1 else (CV2_PE if n < N_PE else CV2[width(n)])
+            if n < N1:
+                return CV1
+            return CV2_PE if by_pe(n) else CV2[width(n)]
+
+        def by_pe(n):
+            return n < N1 or (UNITS2[n - N1][0] == 0 and UNITS2[n - N1][1] < E_PE)
 
         def pe_regroup(n):
             cv = split(n)
@@ -103,12 +112,12 @@ def tile_moelayer_pa_kernel(tc, x, r, Wg, Wu, Wd, out):
             grp_tiles[n] = g
             src = source(n)
             cv = split(n)
-            cs = cv + PE_COLS if n < N_PE else cv
+            cs = cv + PE_COLS if by_pe(n) else cv
             nc.scalar.copy(
                 out=g[:, cs:w, :].rearrange("p (c i) t -> p c t i", i=4),
                 in_=src[:, :, cs:w].rearrange("p t (c i) -> p c t i", i=4),
             )
-            if n < N_PE:
+            if by_pe(n):
                 nc.scalar.copy(out=g[:, cv:cs, :], in_=ck_tiles[n][:])
             nc.vector.tensor_copy(
                 out=g[:, 0:cv, :].rearrange("p (c i) t -> p c t i", i=4),
@@ -194,11 +203,11 @@ def tile_moelayer_pa_kernel(tc, x, r, Wg, Wu, Wd, out):
                         stop=(c == 1),
                     )
             else:
-                b, e = divmod(n - N1, E)
+                b, e = UNITS2[n - N1]
                 for a in range(2):
                     if e == 0:
-                        pool = (psg, psu, psg)[b]
-                        acc[(2 + b, 0, a)] = pool.tile([P, BLOCKS[b][1]], F32, name="acc", tag="acc")
+                        pool, tag = ((psg, "acc"), (psu, "acc"), (pst, "tp"))[b]
+                        acc[(2 + b, 0, a)] = pool.tile([P, BLOCKS[b][1]], F32, name="yacc", tag=tag)
                     cols = slice(P * a, P * a + P)
                     nc.tensor.matmul_mx(
                         out=acc[(2 + b, 0, a)][:],
@@ -264,8 +273,9 @@ def tile_moelayer_pa_kernel(tc, x, r, Wg, Wu, Wd, out):
                 regroup(regrouped)
                 if regrouped < 2:
                     x_transposes(regrouped)
-                while pe_done <= min(regrouped + 1, N_PE - 1):
-                    pe_regroup(pe_done)
+                while pe_done <= min(regrouped + 1, NU - 1):
+                    if by_pe(pe_done):
+                        pe_regroup(pe_done)
                     pe_done += 1
                 regrouped += 1
             if n < 0:
@@ -292,9 +302,10 @@ def tile_moelayer_pa_kernel(tc, x, r, Wg, Wu, Wd, out):
             if n % 4 == 1 and 9 <= n <= 37:
                 w_copy((n - 9) // 4, 1)
             for b in range(len(BLOCKS) - 1):
-                if n == N1 + E * b + E + 1:
+                done = N1 + UNITS2.index((b, E - 1))
+                if n == done + 2:
                     y_out(b, 0, nc.scalar.copy, nc.sync)
-                if n == N1 + E * b + E + 2:
+                if n == done + 3:
                     y_out(b, 1, nc.scalar.copy, nc.sync)
         y_out(len(BLOCKS) - 1, 0, nc.vector.tensor_copy, nc.sync)
         y_out(len(BLOCKS) - 1, 1, nc.scalar.copy, nc.scalar)

from contextlib import ExitStack

import concourse.mybir as mybir
from concourse.masks import make_identity

F32 = mybir.dt.float32
BF16 = mybir.dt.bfloat16
U32 = mybir.dt.uint32
U8 = mybir.dt.uint8
FP8X4 = mybir.dt.float8_e4m3fn_x4
SILU = mybir.ActivationFunctionType.Silu
MULT = mybir.AluOpType.mult

P = 128
E = 8
D = 1024
F = 512
NTOK = 256
FLOPS = 2 * NTOK * D * F * E * 2 + 2 * NTOK * E * F * D

N1 = 32
BLOCKS = ((0, 512), (512, 256), (768, 256))
EARLY = 3
ORDER0 = [(0, e) for e in range(E)]
ORDER1 = [(1, e) for e in range(E)]
UNITS2 = ORDER0[: E - EARLY] + ORDER1[:EARLY] + ORDER0[E - EARLY :] + ORDER1[EARLY:] + [(2, e) for e in range(E)]
NU = N1 + len(UNITS2)
RAW_BUFS = 16
CV1 = 216
CV2 = {512: 264, 256: 136}
CV2_PE = 208
E_PE = 6
PE_COLS = 128
MANUAL = True


def tile_moelayer_pa_kernel(tc, x, r, Wg, Wu, Wd, out):
    nc = tc.nc
    with ExitStack() as ctx:
        const = ctx.enter_context(tc.tile_pool(name="const", bufs=1))
        rawa = ctx.enter_context(tc.tile_pool(name="rawa", bufs=RAW_BUFS))
        rawd = ctx.enter_context(tc.tile_pool(name="rawd", bufs=E))
        grp = ctx.enter_context(tc.tile_pool(name="grp", bufs=6))
        cod = ctx.enter_context(tc.tile_pool(name="cod", bufs=8))
        act = ctx.enter_context(tc.tile_pool(name="act", bufs=3))
        yst = ctx.enter_context(tc.tile_pool(name="yst", bufs=6))
        psg = ctx.enter_context(tc.psum_pool(name="psg", bufs=2))
        psu = ctx.enter_context(tc.psum_pool(name="psu", bufs=2))
        pst = ctx.enter_context(tc.psum_pool(name="pst", bufs=2))
        psc = ctx.enter_context(tc.psum_pool(name="psc", bufs=2))
        if MANUAL:
            ctx.enter_context(tc.manual_schedule())

        raw_tiles = {}
        grp_tiles = {}
        code_tiles = {}
        acc = {}
        sg_tiles = {}
        w_tiles = {}
        wt_tiles = {}
        wg_tiles = {}
        ck_tiles = {}

        def load(n):
            if n < N1:
                e, i = divmod(n, 4)
                src = (Wg if i < 2 else Wu)[e]
                c = i % 2
                t = rawa.tile([P, 4, F], BF16, name="rawa", tag="rawa")
                nc.sync.dma_start(
                    out=t[:], in_=src[512 * c : 512 * c + 512, :].rearrange("(p j) f -> p j f", j=4)
                )
                raw_tiles[n] = t
            else:
                e = n - N1
                t = rawd.tile([P, 4, D], BF16, name="rawd", tag="rawd")
                nc.sync.dma_start(out=t[:], in_=Wd[e].rearrange("(p t) d -> p t d", t=4))
                raw_tiles[n] = t

        def width(n):
            return F if n < N1 else BLOCKS[UNITS2[n - N1][0]][1]

        def source(n):
            if n < N1:
                return raw_tiles[n][:]
            b, e = UNITS2[n - N1]
            return raw_tiles[N1 + e][:, :, BLOCKS[b][0] : BLOCKS[b][0] + BLOCKS[b][1]]

        def split(n):
            if n < N1:
                return CV1
            return CV2_PE if by_pe(n) else CV2[width(n)]

        def by_pe(n):
            return n < N1 or (UNITS2[n - N1][0] == 0 and UNITS2[n - N1][1] < E_PE)

        def pe_regroup(n):
            cv = split(n)
            ck = psc.tile([P, PE_COLS, 4], BF16, name="ck", tag="ck")
            nc.tensor.matmul(
                out=ck[:].rearrange("p w (u v) -> p u w v", u=2),
                lhsT=ident_b[:],
                rhs=source(n)[:, :, cv : cv + PE_COLS].rearrange("p (u v) w -> p u w v", u=2),
                start=True,
                stop=True,
            )
            ck_tiles[n] = ck

        def regroup(n):
            w = width(n)
            g = grp.tile([P, w, 4], BF16, name="grp", tag="grp", align_bytes=64)
            grp_tiles[n] = g
            src = source(n)
            cv = split(n)
            cs = cv + PE_COLS if by_pe(n) else cv
            nc.scalar.copy(
                out=g[:, cs:w, :].rearrange("p (c i) t -> p c t i", i=4),
                in_=src[:, :, cs:w].rearrange("p t (c i) -> p c t i", i=4),
            )
            if by_pe(n):
                nc.scalar.copy(out=g[:, cv:cs, :], in_=ck_tiles[n][:])
            nc.vector.tensor_copy(
                out=g[:, 0:cv, :].rearrange("p (c i) t -> p c t i", i=4),
                in_=src[:, :, 0:cv].rearrange("p t (c i) -> p c t i", i=4),
            )
            nxt = n + RAW_BUFS
            if nxt < N1:
                load(nxt)
            elif nxt == N1:
                for e in range(E):
                    load(N1 + e)

        def quantise(n):
            codes = cod.tile([P, width(n)], U32, name="codes", tag="codes", align_bytes=64)
            plane = cod.tile([P, width(n)], U8, name="plane", tag="plane", align_bytes=64)
            nc.vector.quantize_mx(
                out=codes[:].bitcast(FP8X4),
                scales=plane[:],
                in_=grp_tiles[n][:].rearrange("p w t -> p (w t)"),
            )
            code_tiles[n] = (codes, plane)

        ident_f = const.tile([P, P], F32, name="ident_f")
        make_identity(nc, ident_f[:])
        ident_b = const.tile([P, P], BF16, name="ident_b")
        make_identity(nc, ident_b[:])
        r_sb = const.tile([P, 2, E], BF16, name="r_sb")
        nc.scalar.dma_start(out=r_sb[:], in_=r.rearrange("(a p) e -> p a e", a=2))
        warm = const.tile([P, 1], F32, name="warm")
        nc.vector.memset(warm[:], 0.0)
        nc.scalar.activation(out=warm[:], in_=warm[:], func=SILU)
        x_sb = const.tile([P, 2, D], BF16, name="x_sb")
        load(0)
        nc.sync.dma_start(out=x_sb[:], in_=x.rearrange("b t d -> t b d"))
        for n in range(1, RAW_BUFS):
            load(n)

        r32 = const.tile([P, 2, E], F32, name="r32")
        nc.vector.tensor_copy(out=r32[:], in_=r_sb[:])

        xg = const.tile([P, 2, NTOK, 4], BF16, name="xg", align_bytes=64)
        xc = const.tile([P, 2 * NTOK], U32, name="xc", align_bytes=64)
        xs = const.tile([P, 2 * NTOK], U8, name="xs", align_bytes=64)
        wc = const.tile([P, E, NTOK], U32, name="wc", align_bytes=64)
        ws = const.tile([P, E, NTOK], U8, name="ws", align_bytes=64)

        def x_transposes(c):
            xw = x_sb[:].bitcast(F32).rearrange("p a (c q u) -> p a c u q", c=2, u=2)
            xg32 = xg[:].bitcast(F32)
            xt = pst.tile([P, 2, 2, P], F32, name="xt", tag="tp")
            for a in range(2):
                for u in range(2):
                    nc.tensor.transpose(out=xt[:, a, u, :], in_=xw[:, a, c, u, :], identity=ident_f[:])
            nc.scalar.copy(
                out=xg32[:, c].rearrange("p (a q) u -> p a q u", a=2),
                in_=xt[:].rearrange("p a u q -> p a q u"),
            )

        def x_quantise():
            nc.vector.quantize_mx(
                out=xc[:].bitcast(FP8X4),
                scales=xs[:],
                in_=xg[:].rearrange("p c n t -> p (c n t)"),
            )

        def matmuls(n):
            codes, plane = code_tiles[n]
            if n < N1:
                e, i = divmod(n, 4)
                c = i % 2
                for a in range(2):
                    if c == 0:
                        pool = psg if i < 2 else psu
                        acc[(i // 2, e, a)] = pool.tile([P, F], F32, name="acc", tag="acc")
                    cols = slice(NTOK * c + P * a, NTOK * c + P * a + P)
                    nc.tensor.matmul_mx(
                        out=acc[(i // 2, e, a)][:],
                        lhsT=xc[:, cols].bitcast(FP8X4),
                        lhsT_scale=xs[:, cols],
                        rhs=codes[:].bitcast(FP8X4),
                        rhs_scale=plane[:],
                        start=(c == 0),
                        stop=(c == 1),
                    )
            else:
                b, e = UNITS2[n - N1]
                for a in range(2):
                    if e == 0:
                        pool, tag = ((psg, "acc"), (psu, "acc"), (pst, "tp"))[b]
                        acc[(2 + b, 0, a)] = pool.tile([P, BLOCKS[b][1]], F32, name="yacc", tag=tag)
                    cols = slice(P * a, P * a + P)
                    nc.tensor.matmul_mx(
                        out=acc[(2 + b, 0, a)][:],
                        lhsT=wc[:, e, cols].bitcast(FP8X4),
                        lhsT_scale=ws[:, e, cols],
                        rhs=codes[:].bitcast(FP8X4),
                        rhs_scale=plane[:],
                        start=(e == 0),
                        stop=(e == E - 1),
                    )

        def silu(e, a):
            sg = act.tile([P, F], F32, name="sg", tag="sg")
            nc.scalar.activation(out=sg[:], in_=acc[(0, e, a)][:], func=SILU)
            sg_tiles[(e, a)] = sg

        def combine(e, a):
            w = act.tile([P, F], BF16, name="w", tag="w")
            nc.vector.scalar_tensor_tensor(
                out=w[:],
                in0=sg_tiles[(e, a)][:],
                scalar=r32[:, a, e : e + 1],
                in1=acc[(1, e, a)][:],
                op0=MULT,
                op1=MULT,
            )
            w_tiles[(e, a)] = w

        def w_transposes(e):
            wt = pst.tile([P, 2, 2, P], F32, name="wt", tag="tp")
            for a in range(2):
                words = w_tiles[(e, a)][:].bitcast(F32).rearrange("p (q u) -> p u q", u=2)
                for u in range(2):
                    nc.tensor.transpose(out=wt[:, a, u, :], in_=words[:, u, :], identity=ident_f[:])
            wt_tiles[e] = wt

        def w_copy(e, a):
            if a == 0:
                wg_tiles[e] = act.tile([P, NTOK, 4], BF16, name="wg", tag="wg", align_bytes=64)
            nc.scalar.copy(
                out=wg_tiles[e][:].bitcast(F32)[:, P * a : P * a + P, :],
                in_=wt_tiles[e][:, a].rearrange("p u q -> p q u"),
            )

        def w_quantise(e):
            nc.vector.quantize_mx(
                out=wc[:, e, :].bitcast(FP8X4),
                scales=ws[:, e, :],
                in_=wg_tiles[e][:].rearrange("p n t -> p (n t)"),
            )

        def y_out(b, a, copy, queue):
            y = yst.tile([P, BLOCKS[b][1]], F32, name="y", tag="y")
            copy(out=y[:], in_=acc[(2 + b, 0, a)][:])
            queue.dma_start(out=out[a][:, BLOCKS[b][0] : BLOCKS[b][0] + BLOCKS[b][1]], in_=y[:])

        regrouped = 0
        pe_regroup(0)
        pe_done = 1
        for n in range(-1, NU):
            ahead = 1 if n < 0 else min(n, 2)
            while regrouped <= min(n + ahead, NU - 1):
                regroup(regrouped)
                if regrouped < 2:
                    x_transposes(regrouped)
                while pe_done <= min(regrouped + 1, NU - 1):
                    if by_pe(pe_done):
                        pe_regroup(pe_done)
                    pe_done += 1
                regrouped += 1
            if n < 0:
                continue
            if n % 4 == 1 and 5 <= n <= 33:
                combine((n - 5) // 4, 0)
            if n % 4 == 2 and 6 <= n <= 34:
                combine((n - 6) // 4, 1)
                w_transposes((n - 6) // 4)
            quantise(n)
            if n == 1:
                x_quantise()
                matmuls(0)
            if n % 4 == 3 and 11 <= n <= 39:
                w_quantise((n - 11) // 4)
            if n >= 1:
                matmuls(n)
            if n < N1 and n % 4 == 2:
                silu(n // 4, 0)
            if n < N1 and n % 4 == 3:
                silu(n // 4, 1)
            if n % 4 == 0 and 8 <= n <= 36:
                w_copy((n - 8) // 4, 0)
            if n % 4 == 1 and 9 <= n <= 37:
                w_copy((n - 9) // 4, 1)
            for b in range(len(BLOCKS) - 1):
                done = N1 + UNITS2.index((b, E - 1))
                if n == done + 2:
                    y_out(b, 0, nc.scalar.copy, nc.sync)
                if n == done + 3:
                    y_out(b, 1, nc.scalar.copy, nc.sync)
        y_out(len(BLOCKS) - 1, 0, nc.vector.tensor_copy, nc.sync)
        y_out(len(BLOCKS) - 1, 1, nc.scalar.copy, nc.scalar)
